import numpy as np
import ml_dtypes


def mxq(x, axis, fmt="e4m3"):
    dtype, down = {"e4m3": (ml_dtypes.float8_e4m3fn, 7), "e5m2": (ml_dtypes.float8_e5m2, 14)}[fmt]
    v = np.moveaxis(np.asarray(x, np.float32).astype(ml_dtypes.bfloat16).astype(np.float64), axis, -1)
    blocks = v.reshape(v.shape[:-1] + (-1, 32))
    amax = np.abs(blocks).max(-1, keepdims=True)
    byte = np.maximum(np.where(amax > 0, np.frexp(amax)[1] - 1 + 127, 0) - down, 1)
    scale = np.exp2(byte - 127.0)
    codes = (blocks / scale).astype(np.float32).astype(dtype).astype(np.float64)
    return np.moveaxis((codes * scale).reshape(v.shape), -1, axis)


WIDE = False


def mx_kscale(k):
    if not WIDE:
        return np.ones(k)
    levels = np.array([10, -10, 5, -5, 0])
    a = np.random.permutation(np.resize(levels, k // 512 * 4)).reshape(k // 512, 4)
    idx = np.arange(k)
    return np.exp2(a[idx // 512, idx % 128 // 32])


BF16 = ml_dtypes.bfloat16


def bf(x):
    return np.asarray(x, np.float32).astype(BF16)


def f64(x):
    return np.asarray(x).astype(np.float64)


B, N_I, N_H1, N_H2, N_H3, N_H4 = 512, 1024, 1024, 1024, 2048, 1024
K2 = N_H1 + N_H2


def sigmoid(v):
    return 1.0 / (1.0 + np.exp(-v))


def setup_inputs():
    s = mx_kscale(K2)

    def w(gain):
        return bf(np.random.standard_normal((N_H2, K2)) * gain / np.sqrt(K2) / s[None, :])

    def b():
        return bf(np.random.standard_normal(N_H2) * 0.3)

    return {"h1": bf(np.random.standard_normal((B, N_H1)) * 0.3 * s[:N_H1]),
            "hidden2": bf(np.random.standard_normal((B, N_H2)) * s[N_H1:]),
            "cell2": bf(np.random.standard_normal((B, N_H2))),
            "Wf2": w(1.0), "bf2": b(), "Wi2": w(1.0), "bi2": b(),
            "Wc2": w(5.0 / 3.0), "bc2": b(), "Wo2": w(1.0), "bo2": b(),
            "W3": bf(np.random.standard_normal((N_H3, N_H2)) * 3.0 / np.sqrt(N_H2)),
            "b3": bf(np.random.standard_normal(N_H3) * 0.3)}


def reference(h1, hidden2, cell2, Wf2, bf2, Wi2, bi2, Wc2, bc2, Wo2, bo2, W3, b3):
    zq = mxq(np.concatenate([f64(h1), f64(hidden2)], axis=1), 1, "e4m3")
    f = sigmoid((zq @ mxq(f64(Wf2), 1, "e4m3").T) + f64(bf2))
    i = sigmoid((zq @ mxq(f64(Wi2), 1, "e4m3").T) + f64(bi2))
    cand = np.tanh((zq @ mxq(f64(Wc2), 1, "e4m3").T) + f64(bc2))
    o = sigmoid((zq @ mxq(f64(Wo2), 1, "e4m3").T) + f64(bo2))
    h2 = o * np.tanh(cand)
    c2 = f * f64(cell2) + cand * i
    out3 = np.maximum((mxq(h2, 1, "e4m3") @ mxq(f64(W3), 1, "e4m3").T) + f64(b3), 0.0)
    return out3, h2, c2

@@ -1,0 +1,285 @@
+from contextlib import ExitStack
+
+import concourse.mybir as mybir
+from concourse.masks import make_identity
+
+F32 = mybir.dt.float32
+BF16 = mybir.dt.bfloat16
+I32 = mybir.dt.int32
+U32 = mybir.dt.uint32
+U8 = mybir.dt.uint8
+FP8X4 = mybir.dt.float8_e4m3fn_x4
+ACT = mybir.ActivationFunctionType
+
+P = 128
+TOKENS = 512
+TOKEN_TILES = TOKENS // P
+JOINED = 2048
+FEATURES = 1024
+OUTS = 2048
+K_PASS = 512
+BANK = 512
+
+PANEL = 4096
+PANEL_WORDS = PANEL // 4
+SLICES = PANEL_WORDS // P
+PANEL_BANKS = 4
+FEATURES_PER_PANEL = 256
+FEATURE_GROUPS = FEATURES // FEATURES_PER_PANEL
+RAW_BUFS = 5
+
+GATES = ("cand", "o", "f", "i")
+
+FLOPS = 2 * TOKENS * JOINED * 4 * FEATURES + 2 * TOKENS * FEATURES * OUTS
+
+
+def tile_quest_pb_kernel(
+    tc, h1, hidden2, cell2, Wf2, bf2, Wi2, bi2, Wc2, bc2, Wo2, bo2, W3, b3, out_0, out_1, out_2
+):
+    nc = tc.nc
+    out3_dram, h2_dram, c2_dram = out_0, out_1, out_2
+    gate_weight = {"cand": Wc2, "o": Wo2, "f": Wf2, "i": Wi2}
+    gate_bias_dram = {"cand": bc2, "o": bo2, "f": bf2, "i": bi2}
+    gate_func = {"cand": ACT.Tanh, "o": ACT.Sigmoid, "f": ACT.Sigmoid, "i": ACT.Sigmoid}
+
+    panels = [("z", 0), ("z", 1)]
+    for c in range(FEATURE_GROUPS):
+        panels.extend([("cand", c), ("o", c)])
+    for c in range(FEATURE_GROUPS):
+        panels.extend([("f", c), ("i", c), ("w3", c)])
+    n_panels = len(panels)
+
+    with ExitStack() as ctx:
+        keep = ctx.enter_context(tc.tile_pool(name="keep", bufs=1))
+        raw_pool = ctx.enter_context(tc.tile_pool(name="raw", bufs=RAW_BUFS))
+        grouped_pool = ctx.enter_context(tc.tile_pool(name="grouped", bufs=2))
+        operand_pool = ctx.enter_context(tc.tile_pool(name="operand", bufs=2))
+        gate_pool = ctx.enter_context(tc.tile_pool(name="gate", bufs=2))
+        rows_pool = ctx.enter_context(tc.tile_pool(name="rows", bufs=2))
+        y_pool = ctx.enter_context(tc.tile_pool(name="y", bufs=TOKEN_TILES))
+        flip_pool = ctx.enter_context(tc.psum_pool(name="flip", bufs=4))
+        acc_pool = ctx.enter_context(tc.psum_pool(name="acc", bufs=4))
+        ctx.enter_context(tc.manual_schedule())
+
+        ident_f32 = keep.tile([P, P], F32)
+        make_identity(nc, ident_f32[:])
+        ident_bf16 = keep.tile([P, P], BF16)
+        make_identity(nc, ident_bf16[:])
+
+        warm = keep.tile([P, 1], F32)
+
+        bias_rows = keep.tile([P, FEATURES_PER_PANEL], BF16)
+        gate_bias = keep.tile([P, 2, len(GATES) * FEATURE_GROUPS], F32)
+        nc.vector.memset(bias_rows[:].bitcast(I32), 0)
+        nc.vector.memset(warm[:], 0.0)
+        for gate_no, gate in enumerate(GATES):
+            nc.scalar.dma_start(
+                out=bias_rows[FEATURE_GROUPS * gate_no : FEATURE_GROUPS * (gate_no + 1), :],
+                in_=gate_bias_dram[gate].rearrange("(c x) -> c x", x=FEATURES_PER_PANEL),
+            )
+        nc.scalar.activation(out=warm[:], in_=warm[:], func=ACT.Sigmoid)
+
+        cell_rows = keep.tile([P, TOKEN_TILES, FEATURES], BF16)
+        b3_all = keep.tile([P, OUTS], BF16)
+
+        z_codes = [keep.tile([P, PANEL_WORDS], U32, name="z_codes%d" % n, align_bytes=64) for n in range(2)]
+        z_scales = [keep.tile([P, PANEL_WORDS], U8, name="z_scales%d" % n, align_bytes=64) for n in range(2)]
+        h2_passes = FEATURES // K_PASS
+        h2_grouped = [keep.tile([P, 4 * TOKENS], BF16, name="h2_grouped%d" % g, align_bytes=64) for g in range(h2_passes)]
+        h2_codes = [keep.tile([P, TOKENS], U32, name="h2_codes%d" % g, align_bytes=64) for g in range(h2_passes)]
+        h2_scales = [keep.tile([P, TOKENS], U8, name="h2_scales%d" % g, align_bytes=64) for g in range(h2_passes)]
+        cand = [keep.tile([P, 2, TOKENS], F32, name="cand%d" % c) for c in range(FEATURE_GROUPS)]
+
+        def load_panel(kind, n):
+            raw = raw_pool.tile([P, PANEL], BF16)
+            if kind in gate_weight:
+                rows = gate_weight[kind][FEATURES_PER_PANEL * n : FEATURES_PER_PANEL * (n + 1), :]
+                nc.sync.dma_start(out=raw[:], in_=rows.rearrange("(p e) k -> p (e k)", e=2))
+            else:
+                rows = W3[BANK * n : BANK * (n + 1), :] if kind == "w3" else (h1, hidden2)[n]
+                nc.sync.dma_start(
+                    out=raw[:].rearrange("p (j k) -> p j k", j=4), in_=rows.rearrange("(j p) k -> p j k", p=P)
+                )
+            return raw
+
+        def transpose_panel(kind, raw):
+            row_tiles = 2 if kind in gate_weight else 4
+            words = raw[:].bitcast(F32).rearrange("p (j g u w) -> p j g u w", j=row_tiles, u=2, w=P)
+            grouped = grouped_pool.tile([P, PANEL], BF16, align_bytes=64)
+            grouped_words = grouped[:].bitcast(F32).rearrange("q (s r u) -> q s r u", s=SLICES, u=2)
+            for bank_no in range(PANEL_BANKS):
+                flip = flip_pool.tile([P, 2, 2, P], F32, tag="flip")
+                for half in range(2):
+                    g, j = divmod(2 * bank_no + half, row_tiles)
+                    for u in range(2):
+                        nc.tensor.transpose(flip[:, half, u, :], words[:, j, g, u, :], ident_f32[:])
+                empty_bank = nc.vector.tensor_copy if bank_no == PANEL_BANKS - 1 else nc.scalar.copy
+                empty_bank(
+                    out=grouped_words[:, 2 * bank_no : 2 * bank_no + 2, :, :],
+                    in_=flip[:].rearrange("q s u r -> q s r u"),
+                )
+            return grouped
+
+        def quantise(codes, scales, grouped):
+            nc.vector.quantize_mx(out=codes[:].bitcast(FP8X4), scales=scales[:], in_=grouped[:])
+
+        def gate_matmuls(kind, c, codes, scales, gate_out):
+            bias_col = FEATURE_GROUPS * GATES.index(kind) + c
+            for e in range(2):
+                acc = acc_pool.tile([P, TOKENS], F32)
+                passes = JOINED // K_PASS
+                for g in range(passes):
+                    w_cols = slice((2 * g + e) * P, (2 * g + e + 1) * P)
+                    z_cols = slice((g % 2) * TOKENS, (g % 2 + 1) * TOKENS)
+                    nc.tensor.matmul_mx(
+                        out=acc[:],
+                        lhsT=codes[:, w_cols].bitcast(FP8X4),
+                        lhsT_scale=scales[:, w_cols],
+                        rhs=z_codes[g // 2][:, z_cols].bitcast(FP8X4),
+                        rhs_scale=z_scales[g // 2][:, z_cols],
+                        start=(g == 0),
+                        stop=(g == passes - 1),
+                    )
+                nc.scalar.activation(
+                    out=gate_out[:, e, :],
+                    in_=acc[:],
+                    func=gate_func[kind],
+                    bias=gate_bias[:, e, bias_col : bias_col + 1],
+                    scale=1.0,
+                )
+
+        def relu_layer_matmuls(n, codes, scales):
+            sums = []
+            for j in range(TOKEN_TILES):
+                acc = acc_pool.tile([P, BANK], F32)
+                tokens = slice(j * P, (j + 1) * P)
+                for g in range(h2_passes):
+                    w_cols = slice(g * BANK, (g + 1) * BANK)
+                    nc.tensor.matmul_mx(
+                        out=acc[:],
+                        lhsT=h2_codes[g][:, tokens].bitcast(FP8X4),
+                        lhsT_scale=h2_scales[g][:, tokens],
+                        rhs=codes[:, w_cols].bitcast(FP8X4),
+                        rhs_scale=scales[:, w_cols],
+                        start=(g == 0),
+                        stop=(g == h2_passes - 1),
+                    )
+                y = y_pool.tile([P, BANK], F32)
+                nc.vector.tensor_add(out=y[:], in0=acc[:], in1=b3_all[:, n * BANK : (n + 1) * BANK])
+                sums.append(y)
+            return sums
+
+        def relu_and_store(n, sums):
+            for j, y in enumerate(sums):
+                nc.scalar.activation(out=y[:], in_=y[:], func=ACT.Relu)
+                nc.sync.dma_start(out=out3_dram[j * P : (j + 1) * P, n * BANK : (n + 1) * BANK], in_=y[:])
+
+        def transpose_biases():
+            bias_flip = flip_pool.tile([P, 2, P], BF16, tag="flip")
+            by_parity = bias_rows[:].rearrange("r (p e) -> r e p", e=2)
+            for e in range(2):
+                nc.tensor.transpose(bias_flip[:, e, :], by_parity[:, e, :], ident_bf16[:])
+            nc.vector.tensor_copy(out=gate_bias[:], in_=bias_flip[:, :, 0 : len(GATES) * FEATURE_GROUPS])
+
+        def transpose_cell(c):
+            cell_flip = flip_pool.tile([P, 2, TOKENS], BF16, tag="flip")
+            by_parity = cell_rows[:].rearrange("t j (c p e) -> t j c e p", c=FEATURE_GROUPS, e=2)
+            for e in range(2):
+                for j in range(TOKEN_TILES):
+                    nc.tensor.transpose(cell_flip[:, e, j * P : (j + 1) * P], by_parity[:, j, c, e, :], ident_bf16[:])
+            return cell_flip
+
+        def transpose_back_and_store(c, by_feature, dram):
+            rows = rows_pool.tile([P, TOKEN_TILES, FEATURES_PER_PANEL], F32)
+            for pair in range(TOKEN_TILES // 2):
+                back = flip_pool.tile([P, 2, 2, P], F32, tag="flip")
+                for half in range(2):
+                    j = 2 * pair + half
+                    for e in range(2):
+                        nc.tensor.transpose(back[:, half, e, :], by_feature[:, e, j * P : (j + 1) * P], ident_f32[:])
+                nc.scalar.copy(
+                    out=rows[:, 2 * pair : 2 * pair + 2, :].rearrange("t j (p e) -> t j p e", e=2),
+                    in_=back[:].rearrange("t j e p -> t j p e"),
+                )
+            nc.sync.dma_start(
+                out=dram[:, FEATURES_PER_PANEL * c : FEATURES_PER_PANEL * (c + 1)].rearrange("(j t) x -> t j x", t=P),
+                in_=rows[:],
+            )
+
+        nothing = ("none", 0)
+        raw = {}
+        operand = {}
+        live = {}
+        for r in range(RAW_BUFS - 1):
+            raw[r] = load_panel(*panels[r])
+
+        for r in range(n_panels + 2):
+            new_kind, new_n = panels[r] if r < n_panels else nothing
+            mul_kind, mul_n = panels[r - 1] if 1 <= r <= n_panels else nothing
+            done_kind, done_n = panels[r - 2] if 2 <= r else nothing
+            back_kind, back_n = panels[r - 3] if 3 <= r else nothing
+
+            ahead = r + RAW_BUFS - 1
+            if ahead < n_panels:
+                raw[ahead] = load_panel(*panels[ahead])
+            if (new_kind, new_n) == ("cand", 0):
+                nc.sync.dma_start(out=cell_rows[:], in_=cell2.rearrange("(j t) x -> t j x", t=P))
+                nc.sync.dma_start(out=b3_all[:], in_=b3.partition_broadcast(P))
+
+            if (mul_kind, mul_n) == ("cand", 0):
+                transpose_biases()
+            if back_kind == "o":
+                transpose_back_and_store(back_n, live["h2_t"], h2_dram)
+            if back_kind == "i":
+                transpose_back_and_store(back_n, live["c2_t"], c2_dram)
+            if done_kind == "f":
+                cell_flip = transpose_cell(done_n)
+
+            if done_kind == "o":
+                h2_t = gate_pool.tile([P, 2, TOKENS], F32)
+                nc.vector.tensor_mul(out=h2_t[:], in0=live["o"][:], in1=live["tanh_cand"][:])
+                live["h2_t"] = h2_t
+                g, u = divmod(done_n, 2)
+                nc.vector.tensor_copy(
+                    out=h2_grouped[g][:].rearrange("p (t v) -> p t v", v=4)[:, :, 2 * u : 2 * u + 2],
+                    in_=h2_t[:].rearrange("p e t -> p t e"),
+                )
+            if done_kind == "f":
+                f_cell = gate_pool.tile([P, 2, TOKENS], F32)
+                nc.vector.tensor_mul(out=f_cell[:], in0=live["f"][:], in1=cell_flip[:])
+                live["f_cell"] = f_cell
+            if done_kind == "i":
+                i_cand = gate_pool.tile([P, 2, TOKENS], F32)
+                nc.vector.tensor_mul(out=i_cand[:], in0=live["i"][:], in1=cand[done_n][:])
+                c2_t = gate_pool.tile([P, 2, TOKENS], F32)
+                nc.vector.tensor_add(out=c2_t[:], in0=live["f_cell"][:], in1=i_cand[:])
+                live["c2_t"] = c2_t
+
+            if r < n_panels:
+                grouped = transpose_panel(new_kind, raw[r])
+
+            if done_kind == "w3":
+                relu_and_store(done_n, live["sums"])
+
+            if r < n_panels:
+                if new_kind == "z":
+                    operand[r] = (z_codes[new_n], z_scales[new_n])
+                else:
+                    codes = operand_pool.tile([P, PANEL_WORDS], U32, align_bytes=64)
+                    scales = operand_pool.tile([P, PANEL_WORDS], U8, align_bytes=64)
+                    operand[r] = (codes, scales)
+                quantise(operand[r][0], operand[r][1], grouped)
+            if done_kind == "o" and done_n % 2 == 1:
+                quantise(h2_codes[done_n // 2], h2_scales[done_n // 2], h2_grouped[done_n // 2])
+
+            if mul_kind == "cand":
+                gate_matmuls(mul_kind, mul_n, operand[r - 1][0], operand[r - 1][1], cand[mul_n])
+                tanh_cand = gate_pool.tile([P, 2, TOKENS], F32)
+                nc.scalar.activation(out=tanh_cand[:], in_=cand[mul_n][:], func=ACT.Tanh)
+                live["tanh_cand"] = tanh_cand
+            if mul_kind in ("o", "f", "i"):
+                gate_out = gate_pool.tile([P, 2, TOKENS], F32, tag=mul_kind)
+                gate_matmuls(mul_kind, mul_n, operand[r - 1][0], operand[r - 1][1], gate_out)
+                live[mul_kind] = gate_out
+            if mul_kind == "w3":
+                live["sums"] = relu_layer_matmuls(mul_n, operand[r - 1][0], operand[r - 1][1])

@@ -57,8 +57,7 @@ def tile_quest_pb_kernel(
         gate_pool = ctx.enter_context(tc.tile_pool(name="gate", bufs=2))
         rows_pool = ctx.enter_context(tc.tile_pool(name="rows", bufs=2))
         y_pool = ctx.enter_context(tc.tile_pool(name="y", bufs=TOKEN_TILES))
-        flip_pool = ctx.enter_context(tc.psum_pool(name="flip", bufs=4))
-        acc_pool = ctx.enter_context(tc.psum_pool(name="acc", bufs=4))
+        psum = ctx.enter_context(tc.psum_pool(name="psum", bufs=8))
         ctx.enter_context(tc.manual_schedule())
 
         ident_f32 = keep.tile([P, P], F32)
@@ -102,18 +101,19 @@ def tile_quest_pb_kernel(
                 )
             return raw
 
-        def transpose_panel(kind, raw):
+        def transpose_panel(kind, raw, vector_helps):
             row_tiles = 2 if kind in gate_weight else 4
             words = raw[:].bitcast(F32).rearrange("p (j g u w) -> p j g u w", j=row_tiles, u=2, w=P)
             grouped = grouped_pool.tile([P, PANEL], BF16, align_bytes=64)
             grouped_words = grouped[:].bitcast(F32).rearrange("q (s r u) -> q s r u", s=SLICES, u=2)
             for bank_no in range(PANEL_BANKS):
-                flip = flip_pool.tile([P, 2, 2, P], F32, tag="flip")
+                flip = psum.tile([P, 2, 2, P], F32, tag="bank")
                 for half in range(2):
                     g, j = divmod(2 * bank_no + half, row_tiles)
                     for u in range(2):
                         nc.tensor.transpose(flip[:, half, u, :], words[:, j, g, u, :], ident_f32[:])
-                empty_bank = nc.vector.tensor_copy if bank_no == PANEL_BANKS - 1 else nc.scalar.copy
+                last = bank_no == PANEL_BANKS - 1
+                empty_bank = nc.vector.tensor_copy if last and vector_helps else nc.scalar.copy
                 empty_bank(
                     out=grouped_words[:, 2 * bank_no : 2 * bank_no + 2, :, :],
                     in_=flip[:].rearrange("q s u r -> q s r u"),
@@ -126,7 +126,7 @@ def tile_quest_pb_kernel(
         def gate_matmuls(kind, c, codes, scales, gate_out):
             bias_col = FEATURE_GROUPS * GATES.index(kind) + c
             for e in range(2):
-                acc = acc_pool.tile([P, TOKENS], F32)
+                acc = psum.tile([P, TOKENS], F32, tag="bank")
                 passes = JOINED // K_PASS
                 for g in range(passes):
                     w_cols = slice((2 * g + e) * P, (2 * g + e + 1) * P)
@@ -151,7 +151,7 @@ def tile_quest_pb_kernel(
         def relu_layer_matmuls(n, codes, scales):
             sums = []
             for j in range(TOKEN_TILES):
-                acc = acc_pool.tile([P, BANK], F32)
+                acc = psum.tile([P, BANK], F32, tag="bank")
                 tokens = slice(j * P, (j + 1) * P)
                 for g in range(h2_passes):
                     w_cols = slice(g * BANK, (g + 1) * BANK)
@@ -175,14 +175,14 @@ def tile_quest_pb_kernel(
                 nc.sync.dma_start(out=out3_dram[j * P : (j + 1) * P, n * BANK : (n + 1) * BANK], in_=y[:])
 
         def transpose_biases():
-            bias_flip = flip_pool.tile([P, 2, P], BF16, tag="flip")
+            bias_flip = psum.tile([P, 2, P], BF16, tag="bank")
             by_parity = bias_rows[:].rearrange("r (p e) -> r e p", e=2)
             for e in range(2):
                 nc.tensor.transpose(bias_flip[:, e, :], by_parity[:, e, :], ident_bf16[:])
             nc.vector.tensor_copy(out=gate_bias[:], in_=bias_flip[:, :, 0 : len(GATES) * FEATURE_GROUPS])
 
         def transpose_cell(c):
-            cell_flip = flip_pool.tile([P, 2, TOKENS], BF16, tag="flip")
+            cell_flip = psum.tile([P, 2, TOKENS], BF16, tag="bank")
             by_parity = cell_rows[:].rearrange("t j (c p e) -> t j c e p", c=FEATURE_GROUPS, e=2)
             for e in range(2):
                 for j in range(TOKEN_TILES):
@@ -192,7 +192,7 @@ def tile_quest_pb_kernel(
         def transpose_back_and_store(c, by_feature, dram):
             rows = rows_pool.tile([P, TOKEN_TILES, FEATURES_PER_PANEL], F32)
             for pair in range(TOKEN_TILES // 2):
-                back = flip_pool.tile([P, 2, 2, P], F32, tag="flip")
+                back = psum.tile([P, 2, 2, P], F32, tag="bank")
                 for half in range(2):
                     j = 2 * pair + half
                     for e in range(2):
@@ -256,8 +256,12 @@ def tile_quest_pb_kernel(
                 live["c2_t"] = c2_t
 
             if r < n_panels:
-                grouped = transpose_panel(new_kind, raw[r])
+                grouped = transpose_panel(new_kind, raw[r], vector_helps=(mul_kind != "w3"))
 
+            if done_kind == "cand":
+                tanh_cand = gate_pool.tile([P, 2, TOKENS], F32)
+                nc.scalar.activation(out=tanh_cand[:], in_=cand[done_n][:], func=ACT.Tanh)
+                live["tanh_cand"] = tanh_cand
             if done_kind == "w3":
                 relu_and_store(done_n, live["sums"])
 
@@ -274,9 +278,6 @@ def tile_quest_pb_kernel(
 
             if mul_kind == "cand":
                 gate_matmuls(mul_kind, mul_n, operand[r - 1][0], operand[r - 1][1], cand[mul_n])
-                tanh_cand = gate_pool.tile([P, 2, TOKENS], F32)
-                nc.scalar.activation(out=tanh_cand[:], in_=cand[mul_n][:], func=ACT.Tanh)
-                live["tanh_cand"] = tanh_cand
             if mul_kind in ("o", "f", "i"):
                 gate_out = gate_pool.tile([P, 2, TOKENS], F32, tag=mul_kind)
                 gate_matmuls(mul_kind, mul_n, operand[r - 1][0], operand[r - 1][1], gate_out)

@@ -46,7 +46,10 @@ def tile_quest_pb_kernel(
     for c in range(FEATURE_GROUPS):
         panels.extend([("cand", c), ("o", c)])
     for c in range(FEATURE_GROUPS):
-        panels.extend([("f", c), ("i", c), ("w3", c)])
+        panels.extend([("f", c), ("i", c)])
+        if c > 0:
+            panels.append(("w3", c - 1))
+    panels.append(("w3", FEATURE_GROUPS - 1))
     n_panels = len(panels)
 
     with ExitStack() as ctx:
@@ -56,7 +59,7 @@ def tile_quest_pb_kernel(
         operand_pool = ctx.enter_context(tc.tile_pool(name="operand", bufs=2))
         gate_pool = ctx.enter_context(tc.tile_pool(name="gate", bufs=2))
         rows_pool = ctx.enter_context(tc.tile_pool(name="rows", bufs=2))
-        y_pool = ctx.enter_context(tc.tile_pool(name="y", bufs=TOKEN_TILES))
+        y_pool = ctx.enter_context(tc.tile_pool(name="y", bufs=2 * TOKEN_TILES))
         psum = ctx.enter_context(tc.psum_pool(name="psum", bufs=8))
         ctx.enter_context(tc.manual_schedule())
 
@@ -91,14 +94,20 @@ def tile_quest_pb_kernel(
 
         def load_panel(kind, n):
             raw = raw_pool.tile([P, PANEL], BF16)
-            if kind in gate_weight:
-                rows = gate_weight[kind][FEATURES_PER_PANEL * n : FEATURES_PER_PANEL * (n + 1), :]
-                nc.sync.dma_start(out=raw[:], in_=rows.rearrange("(p e) k -> p (e k)", e=2))
+            if kind == "w3":
+                source = W3[BANK * n : BANK * (n + 1), :].rearrange("(j p) k -> p j k", p=P)
+                target = raw[:].rearrange("p (j k) -> p j k", j=4)
+                for half in range(2):
+                    nc.sync.dma_start(out=target[:, 2 * half : 2 * half + 2, :], in_=source[:, 2 * half : 2 * half + 2, :])
             else:
-                rows = W3[BANK * n : BANK * (n + 1), :] if kind == "w3" else (h1, hidden2)[n]
-                nc.sync.dma_start(
-                    out=raw[:].rearrange("p (j k) -> p j k", j=4), in_=rows.rearrange("(j p) k -> p j k", p=P)
-                )
+                if kind == "z":
+                    source = (h1, hidden2)[n].rearrange("(p j) k -> p (j k)", j=TOKEN_TILES)
+                else:
+                    rows = gate_weight[kind][FEATURES_PER_PANEL * n : FEATURES_PER_PANEL * (n + 1), :]
+                    source = rows.rearrange("(p e) k -> p (e k)", e=2)
+                for half in range(2):
+                    columns = slice(half * PANEL // 2, (half + 1) * PANEL // 2)
+                    nc.sync.dma_start(out=raw[:, columns], in_=source[:, columns])
             return raw
 
         def transpose_panel(kind, raw, vector_helps):
@@ -107,15 +116,17 @@ def tile_quest_pb_kernel(
             grouped = grouped_pool.tile([P, PANEL], BF16, align_bytes=64)
             grouped_words = grouped[:].bitcast(F32).rearrange("q (s r u) -> q s r u", s=SLICES, u=2)
             for bank_no in range(PANEL_BANKS):
+                first, second = divmod(bank_no, 2)
+                first_slice = 2 * bank_no if row_tiles == 2 else 4 * second + 2 * first
                 flip = psum.tile([P, 2, 2, P], F32, tag="bank")
                 for half in range(2):
-                    g, j = divmod(2 * bank_no + half, row_tiles)
+                    j, g = (first, 2 * second + half) if row_tiles == 2 else (2 * first + half, second)
                     for u in range(2):
                         nc.tensor.transpose(flip[:, half, u, :], words[:, j, g, u, :], ident_f32[:])
                 last = bank_no == PANEL_BANKS - 1
                 empty_bank = nc.vector.tensor_copy if last and vector_helps else nc.scalar.copy
                 empty_bank(
-                    out=grouped_words[:, 2 * bank_no : 2 * bank_no + 2, :, :],
+                    out=grouped_words[:, first_slice : first_slice + 2, :, :],
                     in_=flip[:].rearrange("q s u r -> q s r u"),
                 )
             return grouped
@@ -129,7 +140,7 @@ def tile_quest_pb_kernel(
                 acc = psum.tile([P, TOKENS], F32, tag="bank")
                 passes = JOINED // K_PASS
                 for g in range(passes):
-                    w_cols = slice((2 * g + e) * P, (2 * g + e + 1) * P)
+                    w_cols = slice((passes * e + g) * P, (passes * e + g + 1) * P)
                     z_cols = slice((g % 2) * TOKENS, (g % 2 + 1) * TOKENS)
                     nc.tensor.matmul_mx(
                         out=acc[:],
@@ -170,9 +181,10 @@ def tile_quest_pb_kernel(
             return sums
 
         def relu_and_store(n, sums):
+            by_tile = out3_dram[:, n * BANK : (n + 1) * BANK].rearrange("(t j) x -> j t x", j=TOKEN_TILES)
             for j, y in enumerate(sums):
                 nc.scalar.activation(out=y[:], in_=y[:], func=ACT.Relu)
-                nc.sync.dma_start(out=out3_dram[j * P : (j + 1) * P, n * BANK : (n + 1) * BANK], in_=y[:])
+                nc.sync.dma_start(out=by_tile[j], in_=y[:])
 
         def transpose_biases():
             bias_flip = psum.tile([P, 2, P], BF16, tag="bank")
@@ -202,7 +214,7 @@ def tile_quest_pb_kernel(
                     in_=back[:].rearrange("t j e p -> t j p e"),
                 )
             nc.sync.dma_start(
-                out=dram[:, FEATURES_PER_PANEL * c : FEATURES_PER_PANEL * (c + 1)].rearrange("(j t) x -> t j x", t=P),
+                out=dram[:, FEATURES_PER_PANEL * c : FEATURES_PER_PANEL * (c + 1)].rearrange("(t j) x -> t j x", t=P),
                 in_=rows[:],
             )
 
@@ -222,8 +234,8 @@ def tile_quest_pb_kernel(
             ahead = r + RAW_BUFS - 1
             if ahead < n_panels:
                 raw[ahead] = load_panel(*panels[ahead])
-            if (new_kind, new_n) == ("cand", 0):
-                nc.sync.dma_start(out=cell_rows[:], in_=cell2.rearrange("(j t) x -> t j x", t=P))
+            if (new_kind, new_n) == ("cand", 2):
+                nc.sync.dma_start(out=cell_rows[:], in_=cell2.rearrange("(t j) x -> t j x", t=P))
                 nc.sync.dma_start(out=b3_all[:], in_=b3.partition_broadcast(P))
 
             if (mul_kind, mul_n) == ("cand", 0):

@@ -26,7 +26,7 @@ SLICES = PANEL_WORDS // P
 PANEL_BANKS = 4
 FEATURES_PER_PANEL = 256
 FEATURE_GROUPS = FEATURES // FEATURES_PER_PANEL
-RAW_BUFS = 5
+RAW_BUFS = 6
 
 GATES = ("cand", "o", "f", "i")
 
@@ -42,22 +42,32 @@ def tile_quest_pb_kernel(
     gate_bias_dram = {"cand": bc2, "o": bo2, "f": bf2, "i": bi2}
     gate_func = {"cand": ACT.Tanh, "o": ACT.Sigmoid, "f": ACT.Sigmoid, "i": ACT.Sigmoid}
 
-    panels = [("z", 0), ("z", 1)]
-    for c in range(FEATURE_GROUPS):
-        panels.extend([("cand", c), ("o", c)])
-    for c in range(FEATURE_GROUPS):
-        panels.extend([("f", c), ("i", c)])
-        if c > 0:
-            panels.append(("w3", c - 1))
-    panels.append(("w3", FEATURE_GROUPS - 1))
-    n_panels = len(panels)
+    rounds = [
+        ([("z", 0)], []),
+        ([("z", 1)], []),
+        ([("cand", 0)], []),
+        ([("o", 0)], [("cand", 0)]),
+        ([("cand", 1)], [("o", 0)]),
+        ([("o", 1)], [("cand", 1)]),
+        ([("cand", 2), ("o", 2)], [("o", 1)]),
+        ([("cand", 3), ("o", 3)], [("cand", 2), ("o", 2)]),
+        ([("f", 0), ("i", 0)], [("cand", 3), ("o", 3)]),
+        ([("f", 1), ("i", 1)], [("f", 0), ("i", 0)]),
+        ([("f", 2), ("w3", 0)], [("f", 1), ("i", 1)]),
+        ([("i", 2), ("f", 3)], [("f", 2), ("w3", 0)]),
+        ([("i", 3), ("w3", 1)], [("i", 2), ("f", 3)]),
+        ([("w3", 2), ("w3", 3)], [("i", 3), ("w3", 1)]),
+        ([], [("w3", 2)]),
+        ([], [("w3", 3)]),
+    ]
+    panels = [panel for new, mul in rounds for panel in new]
 
     with ExitStack() as ctx:
         keep = ctx.enter_context(tc.tile_pool(name="keep", bufs=1))
         raw_pool = ctx.enter_context(tc.tile_pool(name="raw", bufs=RAW_BUFS))
-        grouped_pool = ctx.enter_context(tc.tile_pool(name="grouped", bufs=2))
-        operand_pool = ctx.enter_context(tc.tile_pool(name="operand", bufs=2))
-        gate_pool = ctx.enter_context(tc.tile_pool(name="gate", bufs=2))
+        grouped_pool = ctx.enter_context(tc.tile_pool(name="grouped", bufs=3))
+        operand_pool = ctx.enter_context(tc.tile_pool(name="operand", bufs=4))
+        gate_pool = ctx.enter_context(tc.tile_pool(name="gate", bufs=3))
         rows_pool = ctx.enter_context(tc.tile_pool(name="rows", bufs=2))
         y_pool = ctx.enter_context(tc.tile_pool(name="y", bufs=2 * TOKEN_TILES))
         psum = ctx.enter_context(tc.psum_pool(name="psum", bufs=8))
@@ -110,7 +120,7 @@ def tile_quest_pb_kernel(
                     nc.sync.dma_start(out=raw[:, columns], in_=source[:, columns])
             return raw
 
-        def transpose_panel(kind, raw, vector_helps):
+        def transpose_panel(kind, raw, vector_banks):
             row_tiles = 2 if kind in gate_weight else 4
             words = raw[:].bitcast(F32).rearrange("p (j g u w) -> p j g u w", j=row_tiles, u=2, w=P)
             grouped = grouped_pool.tile([P, PANEL], BF16, align_bytes=64)
@@ -123,8 +133,7 @@ def tile_quest_pb_kernel(
                     j, g = (first, 2 * second + half) if row_tiles == 2 else (2 * first + half, second)
                     for u in range(2):
                         nc.tensor.transpose(flip[:, half, u, :], words[:, j, g, u, :], ident_f32[:])
-                last = bank_no == PANEL_BANKS - 1
-                empty_bank = nc.vector.tensor_copy if last and vector_helps else nc.scalar.copy
+                empty_bank = nc.vector.tensor_copy if bank_no in vector_banks else nc.scalar.copy
                 empty_bank(
                     out=grouped_words[:, first_slice : first_slice + 2, :, :],
                     in_=flip[:].rearrange("q s u r -> q s r u"),
@@ -133,6 +142,13 @@ def tile_quest_pb_kernel(
 
         def quantise(codes, scales, grouped):
             nc.vector.quantize_mx(out=codes[:].bitcast(FP8X4), scales=scales[:], in_=grouped[:])
+
+        def tanh_of_cand():
+            if "new_cand" in live:
+                c = live.pop("new_cand")
+                tanh_cand = gate_pool.tile([P, 2, TOKENS], F32)
+                nc.scalar.activation(out=tanh_cand[:], in_=cand[c][:], func=ACT.Tanh)
+                live["tanh_cand", c] = tanh_cand
 
         def gate_matmuls(kind, c, codes, scales, gate_out):
             bias_col = FEATURE_GROUPS * GATES.index(kind) + c
@@ -158,8 +174,12 @@ def tile_quest_pb_kernel(
                     bias=gate_bias[:, e, bias_col : bias_col + 1],
                     scale=1.0,
                 )
+                tanh_of_cand()
+            if kind == "cand":
+                live["new_cand"] = c
 
         def relu_layer_matmuls(n, codes, scales):
+            by_tile = out3_dram[:, n * BANK : (n + 1) * BANK].rearrange("(t j) x -> j t x", j=TOKEN_TILES)
             sums = []
             for j in range(TOKEN_TILES):
                 acc = psum.tile([P, BANK], F32, tag="bank")
@@ -178,13 +198,37 @@ def tile_quest_pb_kernel(
                 y = y_pool.tile([P, BANK], F32)
                 nc.vector.tensor_add(out=y[:], in0=acc[:], in1=b3_all[:, n * BANK : (n + 1) * BANK])
                 sums.append(y)
-            return sums
+                if j > 0:
+                    relu_and_store(n, by_tile[j - 1], sums[j - 1])
+                if products and j % 2 == 1:
+                    products.pop(0)()
+            relu_and_store(n, by_tile[TOKEN_TILES - 1], sums[TOKEN_TILES - 1])
 
-        def relu_and_store(n, sums):
-            by_tile = out3_dram[:, n * BANK : (n + 1) * BANK].rearrange("(t j) x -> j t x", j=TOKEN_TILES)
-            for j, y in enumerate(sums):
+        def relu_and_store(n, dram, y):
+            if n == 0:
+                nc.vector.tensor_scalar_max(out=y[:], in0=y[:], scalar1=0.0)
+            else:
                 nc.scalar.activation(out=y[:], in_=y[:], func=ACT.Relu)
-                nc.sync.dma_start(out=by_tile[j], in_=y[:])
+            nc.sync.dma_start(out=dram, in_=y[:])
+
+        def h2_steps(c, o, tanh_cand):
+            g, u = divmod(c, 2)
+            steps = [
+                lambda: nc.vector.tensor_mul(out=o[:], in0=o[:], in1=tanh_cand[:]),
+                lambda: nc.vector.tensor_copy(
+                    out=h2_grouped[g][:].rearrange("p (t v) -> p t v", v=4)[:, :, 2 * u : 2 * u + 2],
+                    in_=o[:].rearrange("p e t -> p t e"),
+                ),
+            ]
+            if u == 1:
+                steps.append(lambda: quantise(h2_codes[g], h2_scales[g], h2_grouped[g]))
+            return steps
+
+        def c2_steps(f_cell, i, cand_c):
+            return [
+                lambda: nc.vector.tensor_mul(out=i[:], in0=i[:], in1=cand_c[:]),
+                lambda: nc.vector.tensor_add(out=f_cell[:], in0=f_cell[:], in1=i[:]),
+            ]
 
         def transpose_biases():
             bias_flip = psum.tile([P, 2, P], BF16, tag="bank")
@@ -218,81 +262,71 @@ def tile_quest_pb_kernel(
                 in_=rows[:],
             )
 
-        nothing = ("none", 0)
         raw = {}
         operand = {}
         live = {}
-        for r in range(RAW_BUFS - 1):
-            raw[r] = load_panel(*panels[r])
+        n_loaded = 0
+        products = []
+        back = []
+        done = []
+        biases_there = False
 
-        for r in range(n_panels + 2):
-            new_kind, new_n = panels[r] if r < n_panels else nothing
-            mul_kind, mul_n = panels[r - 1] if 1 <= r <= n_panels else nothing
-            done_kind, done_n = panels[r - 2] if 2 <= r else nothing
-            back_kind, back_n = panels[r - 3] if 3 <= r else nothing
+        for r, (new, mul) in enumerate(rounds):
+            first_new = panels.index(new[0]) if new else len(panels)
+            while n_loaded < min(first_new + RAW_BUFS, len(panels)):
+                raw[panels[n_loaded]] = load_panel(*panels[n_loaded])
+                n_loaded += 1
+                if panels[n_loaded - 1] == ("o", 3):
+                    nc.sync.dma_start(out=cell_rows[:], in_=cell2.rearrange("(t j) x -> t j x", t=P))
+                    nc.sync.dma_start(out=b3_all[:], in_=b3.partition_broadcast(P))
 
-            ahead = r + RAW_BUFS - 1
-            if ahead < n_panels:
-                raw[ahead] = load_panel(*panels[ahead])
-            if (new_kind, new_n) == ("cand", 2):
-                nc.sync.dma_start(out=cell_rows[:], in_=cell2.rearrange("(t j) x -> t j x", t=P))
-                nc.sync.dma_start(out=b3_all[:], in_=b3.partition_broadcast(P))
-
-            if (mul_kind, mul_n) == ("cand", 0):
+            if mul and not biases_there:
                 transpose_biases()
-            if back_kind == "o":
-                transpose_back_and_store(back_n, live["h2_t"], h2_dram)
-            if back_kind == "i":
-                transpose_back_and_store(back_n, live["c2_t"], c2_dram)
-            if done_kind == "f":
-                cell_flip = transpose_cell(done_n)
+                biases_there = True
+            while back and back[0][0] == r:
+                transpose_back_and_store(*back.pop(0)[1:])
 
-            if done_kind == "o":
-                h2_t = gate_pool.tile([P, 2, TOKENS], F32)
-                nc.vector.tensor_mul(out=h2_t[:], in0=live["o"][:], in1=live["tanh_cand"][:])
-                live["h2_t"] = h2_t
-                g, u = divmod(done_n, 2)
-                nc.vector.tensor_copy(
-                    out=h2_grouped[g][:].rearrange("p (t v) -> p t v", v=4)[:, :, 2 * u : 2 * u + 2],
-                    in_=h2_t[:].rearrange("p e t -> p t e"),
-                )
-            if done_kind == "f":
-                f_cell = gate_pool.tile([P, 2, TOKENS], F32)
-                nc.vector.tensor_mul(out=f_cell[:], in0=live["f"][:], in1=cell_flip[:])
-                live["f_cell"] = f_cell
-            if done_kind == "i":
-                i_cand = gate_pool.tile([P, 2, TOKENS], F32)
-                nc.vector.tensor_mul(out=i_cand[:], in0=live["i"][:], in1=cand[done_n][:])
-                c2_t = gate_pool.tile([P, 2, TOKENS], F32)
-                nc.vector.tensor_add(out=c2_t[:], in0=live["f_cell"][:], in1=i_cand[:])
-                live["c2_t"] = c2_t
+            for kind, c in done:
+                if kind == "f":
+                    cell_flip = transpose_cell(c)
+                    nc.vector.tensor_mul(out=live["f", c][:], in0=live["f", c][:], in1=cell_flip[:])
 
-            if r < n_panels:
-                grouped = transpose_panel(new_kind, raw[r], vector_helps=(mul_kind != "w3"))
+            mul_kinds = [kind for kind, n in mul]
+            vector_banks = () if "w3" in mul_kinds else (1, 3) if len(new) == 2 and "o" in mul_kinds else (3,)
+            grouped = {}
+            for panel in new:
+                grouped[panel] = transpose_panel(panel[0], raw[panel], vector_banks)
 
-            if done_kind == "cand":
-                tanh_cand = gate_pool.tile([P, 2, TOKENS], F32)
-                nc.scalar.activation(out=tanh_cand[:], in_=cand[done_n][:], func=ACT.Tanh)
-                live["tanh_cand"] = tanh_cand
-            if done_kind == "w3":
-                relu_and_store(done_n, live["sums"])
-
-            if r < n_panels:
-                if new_kind == "z":
-                    operand[r] = (z_codes[new_n], z_scales[new_n])
+            for panel in new:
+                if panel[0] == "z":
+                    operand[panel] = (z_codes[panel[1]], z_scales[panel[1]])
                 else:
                     codes = operand_pool.tile([P, PANEL_WORDS], U32, align_bytes=64)
                     scales = operand_pool.tile([P, PANEL_WORDS], U8, align_bytes=64)
-                    operand[r] = (codes, scales)
-                quantise(operand[r][0], operand[r][1], grouped)
-            if done_kind == "o" and done_n % 2 == 1:
-                quantise(h2_codes[done_n // 2], h2_scales[done_n // 2], h2_grouped[done_n // 2])
+                    operand[panel] = (codes, scales)
+            quants = [lambda p=panel: quantise(operand[p][0], operand[p][1], grouped[p]) for panel in new]
+            while products or quants:
+                if products:
+                    products.pop(0)()
+                if quants:
+                    quants.pop(0)()
 
-            if mul_kind == "cand":
-                gate_matmuls(mul_kind, mul_n, operand[r - 1][0], operand[r - 1][1], cand[mul_n])
-            if mul_kind in ("o", "f", "i"):
-                gate_out = gate_pool.tile([P, 2, TOKENS], F32, tag=mul_kind)
-                gate_matmuls(mul_kind, mul_n, operand[r - 1][0], operand[r - 1][1], gate_out)
-                live[mul_kind] = gate_out
-            if mul_kind == "w3":
-                live["sums"] = relu_layer_matmuls(mul_n, operand[r - 1][0], operand[r - 1][1])
+            tanh_of_cand()
+
+            for kind, n in mul:
+                codes, scales = operand[kind, n]
+                if kind == "w3":
+                    relu_layer_matmuls(n, codes, scales)
+                elif kind == "cand":
+                    gate_matmuls(kind, n, codes, scales, cand[n])
+                else:
+                    gate_out = gate_pool.tile([P, 2, TOKENS], F32, tag=kind)
+                    gate_matmuls(kind, n, codes, scales, gate_out)
+                    live[kind, n] = gate_out
+                if kind == "o":
+                    products.extend(h2_steps(n, gate_out, live["tanh_cand", n]))
+                    back.append((r + 2, n, gate_out, h2_dram))
+                if kind == "i":
+                    products.extend(c2_steps(live["f", n], gate_out, cand[n]))
+                    back.append((r + 2, n, live["f", n], c2_dram))
+            done = mul

@@ -54,8 +54,8 @@ def tile_quest_pb_kernel(
         ([("f", 0), ("i", 0)], [("cand", 3), ("o", 3)]),
         ([("f", 1), ("i", 1)], [("f", 0), ("i", 0)]),
         ([("f", 2), ("w3", 0)], [("f", 1), ("i", 1)]),
-        ([("i", 2), ("f", 3)], [("f", 2), ("w3", 0)]),
-        ([("i", 3), ("w3", 1)], [("i", 2), ("f", 3)]),
+        ([("f", 3), ("i", 2)], [("f", 2), ("w3", 0)]),
+        ([("i", 3), ("w3", 1)], [("f", 3), ("i", 2)]),
         ([("w3", 2), ("w3", 3)], [("i", 3), ("w3", 1)]),
         ([], [("w3", 2)]),
         ([], [("w3", 3)]),
@@ -140,8 +140,11 @@ def tile_quest_pb_kernel(
                 )
             return grouped
 
-        def quantise(codes, scales, grouped):
-            nc.vector.quantize_mx(out=codes[:].bitcast(FP8X4), scales=scales[:], in_=grouped[:])
+        def quantise(codes, scales, grouped, parts=1, part=0):
+            words = codes.shape[1] // parts
+            cols = slice(part * words, (part + 1) * words)
+            values = slice(4 * part * words, 4 * (part + 1) * words)
+            nc.vector.quantize_mx(out=codes[:, cols].bitcast(FP8X4), scales=scales[:, cols], in_=grouped[:, values])
 
         def tanh_of_cand():
             if "new_cand" in live:
@@ -202,7 +205,7 @@ def tile_quest_pb_kernel(
                     relu_and_store(n, by_tile[j - 1], sums[j - 1])
                 if products and j % 2 == 1:
                     products.pop(0)()
-            relu_and_store(n, by_tile[TOKEN_TILES - 1], sums[TOKEN_TILES - 1])
+            relu_and_store(n if n < 3 else 0, by_tile[TOKEN_TILES - 1], sums[TOKEN_TILES - 1])
 
         def relu_and_store(n, dram, y):
             if n == 0:
@@ -238,12 +241,11 @@ def tile_quest_pb_kernel(
             nc.vector.tensor_copy(out=gate_bias[:], in_=bias_flip[:, :, 0 : len(GATES) * FEATURE_GROUPS])
 
         def transpose_cell(c):
-            cell_flip = psum.tile([P, 2, TOKENS], BF16, tag="bank")
-            by_parity = cell_rows[:].rearrange("t j (c p e) -> t j c e p", c=FEATURE_GROUPS, e=2)
-            for e in range(2):
-                for j in range(TOKEN_TILES):
-                    nc.tensor.transpose(cell_flip[:, e, j * P : (j + 1) * P], by_parity[:, j, c, e, :], ident_bf16[:])
-            return cell_flip
+            cell_flip = psum.tile([P, TOKENS], F32, tag="bank")
+            words = cell_rows[:].rearrange("t j x -> t (j x)").bitcast(F32).rearrange("t (j c p) -> t j c p", j=TOKEN_TILES, p=P)
+            for j in range(TOKEN_TILES):
+                nc.tensor.transpose(cell_flip[:, j * P : (j + 1) * P], words[:, j, c, :], ident_f32[:])
+            return cell_flip[:].bitcast(BF16).rearrange("p (t e) -> p e t", e=2)
 
         def transpose_back_and_store(c, by_feature, dram):
             rows = rows_pool.tile([P, TOKEN_TILES, FEATURES_PER_PANEL], F32)
@@ -270,32 +272,39 @@ def tile_quest_pb_kernel(
         back = []
         done = []
         biases_there = False
+        early = 0
 
         for r, (new, mul) in enumerate(rounds):
             first_new = panels.index(new[0]) if new else len(panels)
             while n_loaded < min(first_new + RAW_BUFS, len(panels)):
                 raw[panels[n_loaded]] = load_panel(*panels[n_loaded])
                 n_loaded += 1
+                if n_loaded == len(panels):
+                    nc.sync.dma_start(out=b3_all[:], in_=b3.partition_broadcast(P))
                 if panels[n_loaded - 1] == ("o", 3):
                     nc.sync.dma_start(out=cell_rows[:], in_=cell2.rearrange("(t j) x -> t j x", t=P))
-                    nc.sync.dma_start(out=b3_all[:], in_=b3.partition_broadcast(P))
 
-            if mul and not biases_there:
-                transpose_biases()
-                biases_there = True
             while back and back[0][0] == r:
                 transpose_back_and_store(*back.pop(0)[1:])
 
+            for n in range(early):
+                products.pop(0)()
             for kind, c in done:
                 if kind == "f":
-                    cell_flip = transpose_cell(c)
-                    nc.vector.tensor_mul(out=live["f", c][:], in0=live["f", c][:], in1=cell_flip[:])
+                    nc.vector.tensor_mul(out=live["f", c][:], in0=live["f", c][:], in1=live["cell", c])
 
             mul_kinds = [kind for kind, n in mul]
             vector_banks = () if "w3" in mul_kinds else (1, 3) if len(new) == 2 and "o" in mul_kinds else (3,)
             grouped = {}
             for panel in new:
                 grouped[panel] = transpose_panel(panel[0], raw[panel], vector_banks)
+
+            if mul and not biases_there:
+                transpose_biases()
+                biases_there = True
+            for kind, c in mul:
+                if kind == "f":
+                    live["cell", c] = transpose_cell(c)
 
             for panel in new:
                 if panel[0] == "z":
@@ -304,7 +313,11 @@ def tile_quest_pb_kernel(
                     codes = operand_pool.tile([P, PANEL_WORDS], U32, align_bytes=64)
                     scales = operand_pool.tile([P, PANEL_WORDS], U8, align_bytes=64)
                     operand[panel] = (codes, scales)
-            quants = [lambda p=panel: quantise(operand[p][0], operand[p][1], grouped[p]) for panel in new]
+            quants = []
+            for panel in new:
+                parts = 2 if panel == ("cand", 0) else 1
+                for part in range(parts):
+                    quants.append(lambda p=panel, n=parts, part=part: quantise(*operand[p], grouped[p], n, part))
             while products or quants:
                 if products:
                     products.pop(0)()
@@ -330,3 +343,4 @@ def tile_quest_pb_kernel(
                     products.extend(c2_steps(live["f", n], gate_out, cand[n]))
                     back.append((r + 2, n, live["f", n], c2_dram))
             done = mul
+            early = 1 if mul and mul[0][0] == "i" and products else 0

@@ -28,6 +28,7 @@ FEATURES_PER_PANEL = 256
 FEATURE_GROUPS = FEATURES // FEATURES_PER_PANEL
 RAW_BUFS = 6
 
+BACK_BEFORE = ((1, 0), (3, 1))
 GATES = ("cand", "o", "f", "i")
 
 FLOPS = 2 * TOKENS * JOINED * 4 * FEATURES + 2 * TOKENS * FEATURES * OUTS
@@ -42,25 +43,31 @@ def tile_quest_pb_kernel(
     gate_bias_dram = {"cand": bc2, "o": bo2, "f": bf2, "i": bi2}
     gate_func = {"cand": ACT.Tanh, "o": ACT.Sigmoid, "f": ACT.Sigmoid, "i": ACT.Sigmoid}
 
+    def whole(*names):
+        return [("w3" if name[:-1] == "w" else name[:-1], int(name[-1]), None) for name in names]
+
     rounds = [
-        ([("z", 0)], []),
-        ([("z", 1)], []),
-        ([("cand", 0)], []),
-        ([("o", 0)], [("cand", 0)]),
-        ([("cand", 1)], [("o", 0)]),
-        ([("o", 1)], [("cand", 1)]),
-        ([("cand", 2), ("o", 2)], [("o", 1)]),
-        ([("cand", 3), ("o", 3)], [("cand", 2), ("o", 2)]),
-        ([("f", 0), ("i", 0)], [("cand", 3), ("o", 3)]),
-        ([("f", 1), ("i", 1)], [("f", 0), ("i", 0)]),
-        ([("f", 2), ("w3", 0)], [("f", 1), ("i", 1)]),
-        ([("f", 3), ("i", 2)], [("f", 2), ("w3", 0)]),
-        ([("i", 3), ("w3", 1)], [("f", 3), ("i", 2)]),
-        ([("w3", 2), ("w3", 3)], [("i", 3), ("w3", 1)]),
-        ([], [("w3", 2)]),
-        ([], [("w3", 3)]),
+        ([("z", 0, 0), ("z", 1, 0)], []),
+        ([("cand", 0, None)], []),
+        ([("o", 0, None)], [("cand", 0, 0)]),
+        ([("z", 0, 1), ("z", 1, 1)], [("o", 0, 0)]),
+        ([("cand", 1, None)], [("cand", 0, 1), ("o", 0, 1)]),
+        ([("o", 1, None)], whole("cand1")),
+        (whole("cand2", "o2"), whole("o1")),
+        (whole("cand3", "o3"), whole("cand2", "o2")),
+        (whole("f0", "i0"), whole("cand3", "o3")),
+        (whole("f1", "i1"), whole("f0", "i0")),
+        (whole("f2", "w0"), whole("f1", "i1")),
+        (whole("f3", "i2"), whole("f2", "w0")),
+        (whole("i3", "w1"), whole("f3", "i2")),
+        (whole("w2", "w3"), whole("i3", "w1")),
+        ([], whole("w2", "w3")),
     ]
-    panels = [panel for new, mul in rounds for panel in new]
+    new_parts = [part for new, mul in rounds for part in new]
+    panels = []
+    for kind, n, half in new_parts:
+        if (kind, n) not in panels:
+            panels.append((kind, n))
 
     with ExitStack() as ctx:
         keep = ctx.enter_context(tc.tile_pool(name="keep", bufs=1))
@@ -102,30 +109,33 @@ def tile_quest_pb_kernel(
         h2_scales = [keep.tile([P, TOKENS], U8, name="h2_scales%d" % g, align_bytes=64) for g in range(h2_passes)]
         cand = [keep.tile([P, 2, TOKENS], F32, name="cand%d" % c) for c in range(FEATURE_GROUPS)]
 
-        def load_panel(kind, n):
-            raw = raw_pool.tile([P, PANEL], BF16)
+        raw = {}
+        products = []
+        back = []
+
+        def load_half(kind, n, half):
+            if (kind, n) not in raw:
+                raw_tile = raw_pool.tile([P, PANEL], BF16, tag="raw")
+                raw[kind, n] = raw_tile
+            columns = slice(half * PANEL // 2, (half + 1) * PANEL // 2)
             if kind == "w3":
-                source = W3[BANK * n : BANK * (n + 1), :].rearrange("(j p) k -> p j k", p=P)
-                target = raw[:].rearrange("p (j k) -> p j k", j=4)
-                for half in range(2):
-                    nc.sync.dma_start(out=target[:, 2 * half : 2 * half + 2, :], in_=source[:, 2 * half : 2 * half + 2, :])
+                source = W3[BANK * n : BANK * (n + 1), :].rearrange("(j p) k -> p j k", p=P)[:, 2 * half : 2 * half + 2, :]
+                target = raw[kind, n][:, columns].rearrange("p (j k) -> p j k", j=2)
             else:
                 if kind == "z":
-                    source = (h1, hidden2)[n].rearrange("(p j) k -> p (j k)", j=TOKEN_TILES)
+                    rows = (h1, hidden2)[n].rearrange("(p j) k -> p (j k)", j=TOKEN_TILES)
                 else:
                     rows = gate_weight[kind][FEATURES_PER_PANEL * n : FEATURES_PER_PANEL * (n + 1), :]
-                    source = rows.rearrange("(p e) k -> p (e k)", e=2)
-                for half in range(2):
-                    columns = slice(half * PANEL // 2, (half + 1) * PANEL // 2)
-                    nc.sync.dma_start(out=raw[:, columns], in_=source[:, columns])
-            return raw
+                    rows = rows.rearrange("(p e) k -> p (e k)", e=2)
+                source = rows[:, columns]
+                target = raw[kind, n][:, columns]
+            nc.sync.dma_start(out=target, in_=source)
 
-        def transpose_panel(kind, raw, vector_banks):
+        def transpose_banks(kind, raw_tile, grouped, banks, vector_banks):
             row_tiles = 2 if kind in gate_weight else 4
-            words = raw[:].bitcast(F32).rearrange("p (j g u w) -> p j g u w", j=row_tiles, u=2, w=P)
-            grouped = grouped_pool.tile([P, PANEL], BF16, align_bytes=64)
+            words = raw_tile[:].bitcast(F32).rearrange("p (j g u w) -> p j g u w", j=row_tiles, u=2, w=P)
             grouped_words = grouped[:].bitcast(F32).rearrange("q (s r u) -> q s r u", s=SLICES, u=2)
-            for bank_no in range(PANEL_BANKS):
+            for bank_no in banks:
                 first, second = divmod(bank_no, 2)
                 first_slice = 2 * bank_no if row_tiles == 2 else 4 * second + 2 * first
                 flip = psum.tile([P, 2, 2, P], F32, tag="bank")
@@ -138,12 +148,10 @@ def tile_quest_pb_kernel(
                     out=grouped_words[:, first_slice : first_slice + 2, :, :],
                     in_=flip[:].rearrange("q s u r -> q s r u"),
                 )
-            return grouped
 
-        def quantise(codes, scales, grouped, parts=1, part=0):
-            words = codes.shape[1] // parts
-            cols = slice(part * words, (part + 1) * words)
-            values = slice(4 * part * words, 4 * (part + 1) * words)
+        def quantise(codes, scales, grouped, first=0, words=None):
+            cols = slice(first, first + (words or codes.shape[1]))
+            values = slice(4 * cols.start, 4 * cols.stop)
             nc.vector.quantize_mx(out=codes[:, cols].bitcast(FP8X4), scales=scales[:, cols], in_=grouped[:, values])
 
         def tanh_of_cand():
@@ -153,16 +161,20 @@ def tile_quest_pb_kernel(
                 nc.scalar.activation(out=tanh_cand[:], in_=cand[c][:], func=ACT.Tanh)
                 live["tanh_cand", c] = tanh_cand
 
-        def gate_matmuls(kind, c, codes, scales, gate_out):
+        def gate_matmuls(kind, c, half, codes, scales, gate_out):
             bias_col = FEATURE_GROUPS * GATES.index(kind) + c
+            first, width = (0, TOKENS) if half is None else (half * TOKENS // 2, TOKENS // 2)
+            both = None
             for e in range(2):
-                acc = psum.tile([P, TOKENS], F32, tag="bank")
+                if half is None or e == 0:
+                    both = psum.tile([P, BANK], F32, tag="bank")
+                acc = both[:] if half is None else both[:, e * width : (e + 1) * width]
                 passes = JOINED // K_PASS
                 for g in range(passes):
                     w_cols = slice((passes * e + g) * P, (passes * e + g + 1) * P)
-                    z_cols = slice((g % 2) * TOKENS, (g % 2 + 1) * TOKENS)
+                    z_cols = slice((g % 2) * TOKENS + first, (g % 2) * TOKENS + first + width)
                     nc.tensor.matmul_mx(
-                        out=acc[:],
+                        out=acc,
                         lhsT=codes[:, w_cols].bitcast(FP8X4),
                         lhsT_scale=scales[:, w_cols],
                         rhs=z_codes[g // 2][:, z_cols].bitcast(FP8X4),
@@ -171,20 +183,23 @@ def tile_quest_pb_kernel(
                         stop=(g == passes - 1),
                     )
                 nc.scalar.activation(
-                    out=gate_out[:, e, :],
-                    in_=acc[:],
+                    out=gate_out[:, e, first : first + width],
+                    in_=acc,
                     func=gate_func[kind],
                     bias=gate_bias[:, e, bias_col : bias_col + 1],
                     scale=1.0,
                 )
-                tanh_of_cand()
-            if kind == "cand":
+                if half != 0:
+                    tanh_of_cand()
+            if kind == "cand" and half != 0:
                 live["new_cand"] = c
 
         def relu_layer_matmuls(n, codes, scales):
             by_tile = out3_dram[:, n * BANK : (n + 1) * BANK].rearrange("(t j) x -> j t x", j=TOKEN_TILES)
             sums = []
             for j in range(TOKEN_TILES):
+                if (n, j) in BACK_BEFORE and back:
+                    transpose_back_and_store(*back.pop(0)[1:])
                 acc = psum.tile([P, BANK], F32, tag="bank")
                 tokens = slice(j * P, (j + 1) * P)
                 for g in range(h2_passes):
@@ -227,7 +242,11 @@ def tile_quest_pb_kernel(
                 steps.append(lambda: quantise(h2_codes[g], h2_scales[g], h2_grouped[g]))
             return steps
 
-        def c2_steps(f_cell, i, cand_c):
+        def c2_steps(c, f_cell, i, cand_c):
+            if c == FEATURE_GROUPS - 1:
+                nc.gpsimd.tensor_mul(out=i[:], in0=i[:], in1=cand_c[:])
+                nc.gpsimd.tensor_add(out=f_cell[:], in0=f_cell[:], in1=i[:])
+                return []
             return [
                 lambda: nc.vector.tensor_mul(out=i[:], in0=i[:], in1=cand_c[:]),
                 lambda: nc.vector.tensor_add(out=f_cell[:], in0=f_cell[:], in1=i[:]),
@@ -264,24 +283,27 @@ def tile_quest_pb_kernel(
                 in_=rows[:],
             )
 
-        raw = {}
-        operand = {}
+        operand = {("z", n): (z_codes[n], z_scales[n]) for n in range(2)}
+        grouped = {}
         live = {}
         n_loaded = 0
-        products = []
-        back = []
+        unused = list(panels)
+        loads = []
+        for kind, n, half in new_parts:
+            loads.extend([(kind, n, part) for part in range(2) if half in (None, part)])
+        products.clear()
+        back.clear()
         done = []
-        biases_there = False
         early = 0
+        biases_there = False
 
         for r, (new, mul) in enumerate(rounds):
-            first_new = panels.index(new[0]) if new else len(panels)
-            while n_loaded < min(first_new + RAW_BUFS, len(panels)):
-                raw[panels[n_loaded]] = load_panel(*panels[n_loaded])
+            while n_loaded < len(loads) and panels.index(loads[n_loaded][:2]) < panels.index(unused[0]) + RAW_BUFS:
+                load_half(*loads[n_loaded])
                 n_loaded += 1
-                if n_loaded == len(panels):
+                if n_loaded == len(loads):
                     nc.sync.dma_start(out=b3_all[:], in_=b3.partition_broadcast(P))
-                if panels[n_loaded - 1] == ("o", 3):
+                if loads[n_loaded - 1] == ("o", 3, 1):
                     nc.sync.dma_start(out=cell_rows[:], in_=cell2.rearrange("(t j) x -> t j x", t=P))
 
             while back and back[0][0] == r:
@@ -289,35 +311,40 @@ def tile_quest_pb_kernel(
 
             for n in range(early):
                 products.pop(0)()
-            for kind, c in done:
+            for kind, c, half in done:
                 if kind == "f":
                     nc.vector.tensor_mul(out=live["f", c][:], in0=live["f", c][:], in1=live["cell", c])
 
-            mul_kinds = [kind for kind, n in mul]
-            vector_banks = () if "w3" in mul_kinds else (1, 3) if len(new) == 2 and "o" in mul_kinds else (3,)
-            grouped = {}
-            for panel in new:
-                grouped[panel] = transpose_panel(panel[0], raw[panel], vector_banks)
-
+            mul_kinds = [kind for kind, n, half in mul]
+            vector_banks = () if "w3" in mul_kinds else (1, 3) if len(new) == 2 and ("o" in mul_kinds or new[0][0] == "z") else (3,)
+            for kind, n, half in new:
+                if (kind, n) not in grouped:
+                    grouped_tile = grouped_pool.tile([P, PANEL], BF16, align_bytes=64, tag="grouped")
+                    grouped[kind, n] = grouped_tile
+                banks = range(PANEL_BANKS) if half is None else range(2 * half, 2 * half + 2)
+                transpose_banks(kind, raw[kind, n], grouped[kind, n], banks, vector_banks)
+                if half != 0:
+                    unused.remove((kind, n))
             if mul and not biases_there:
                 transpose_biases()
                 biases_there = True
-            for kind, c in mul:
+            for kind, c, half in mul:
                 if kind == "f":
                     live["cell", c] = transpose_cell(c)
 
-            for panel in new:
-                if panel[0] == "z":
-                    operand[panel] = (z_codes[panel[1]], z_scales[panel[1]])
-                else:
+            quants = []
+            for kind, n, half in new:
+                if (kind, n) not in operand:
                     codes = operand_pool.tile([P, PANEL_WORDS], U32, align_bytes=64)
                     scales = operand_pool.tile([P, PANEL_WORDS], U8, align_bytes=64)
-                    operand[panel] = (codes, scales)
-            quants = []
-            for panel in new:
-                parts = 2 if panel == ("cand", 0) else 1
-                for part in range(parts):
-                    quants.append(lambda p=panel, n=parts, part=part: quantise(*operand[p], grouped[p], n, part))
+                    operand[kind, n] = (codes, scales)
+                pieces = [(0, PANEL_WORDS)]
+                if kind == "z":
+                    pieces = [(g * TOKENS + half * TOKENS // 2, TOKENS // 2) for g in range(2)]
+                if (kind, n) == ("cand", 0):
+                    pieces = [(0, PANEL_WORDS // 2), (PANEL_WORDS // 2, PANEL_WORDS // 2)]
+                for piece in pieces:
+                    quants.append(lambda p=(kind, n), piece=piece: quantise(*operand[p], grouped[p], *piece))
             while products or quants:
                 if products:
                     products.pop(0)()
@@ -326,21 +353,22 @@ def tile_quest_pb_kernel(
 
             tanh_of_cand()
 
-            for kind, n in mul:
+            for kind, n, half in mul:
                 codes, scales = operand[kind, n]
                 if kind == "w3":
                     relu_layer_matmuls(n, codes, scales)
-                elif kind == "cand":
-                    gate_matmuls(kind, n, codes, scales, cand[n])
-                else:
+                    continue
+                if kind == "cand":
+                    live["cand", n] = cand[n]
+                elif half != 1:
                     gate_out = gate_pool.tile([P, 2, TOKENS], F32, tag=kind)
-                    gate_matmuls(kind, n, codes, scales, gate_out)
                     live[kind, n] = gate_out
-                if kind == "o":
-                    products.extend(h2_steps(n, gate_out, live["tanh_cand", n]))
-                    back.append((r + 2, n, gate_out, h2_dram))
+                gate_matmuls(kind, n, half, codes, scales, live[kind, n])
+                if kind == "o" and half != 0:
+                    products.extend(h2_steps(n, live["o", n], live["tanh_cand", n]))
+                    back.append((r + 2, n, live["o", n], h2_dram))
                 if kind == "i":
-                    products.extend(c2_steps(live["f", n], gate_out, cand[n]))
+                    products.extend(c2_steps(n, live["f", n], live["i", n], cand[n]))
                     back.append((r + 2, n, live["f", n], c2_dram))
             done = mul
             early = 1 if mul and mul[0][0] == "i" and products else 0

@@ -165,6 +165,7 @@ def tile_quest_pb_kernel(
             bias_col = FEATURE_GROUPS * GATES.index(kind) + c
             first, width = (0, TOKENS) if half is None else (half * TOKENS // 2, TOKENS // 2)
             both = None
+            sums = []
             for e in range(2):
                 if half is None or e == 0:
                     both = psum.tile([P, BANK], F32, tag="bank")
@@ -182,15 +183,18 @@ def tile_quest_pb_kernel(
                         start=(g == 0),
                         stop=(g == passes - 1),
                     )
-                nc.scalar.activation(
-                    out=gate_out[:, e, first : first + width],
-                    in_=acc,
-                    func=gate_func[kind],
-                    bias=gate_bias[:, e, bias_col : bias_col + 1],
-                    scale=1.0,
-                )
-                if half != 0:
-                    tanh_of_cand()
+                sums.append(acc)
+                for n in range(len(sums) if half is None or e == 1 else 0):
+                    feature = e if half is None else n
+                    nc.scalar.activation(
+                        out=gate_out[:, feature, first : first + width],
+                        in_=sums.pop(0),
+                        func=gate_func[kind],
+                        bias=gate_bias[:, feature, bias_col : bias_col + 1],
+                        scale=1.0,
+                    )
+                    if half != 0:
+                        tanh_of_cand()
             if kind == "cand" and half != 0:
                 live["new_cand"] = c
 

@@ -72,7 +72,7 @@ def tile_quest_pb_kernel(
     with ExitStack() as ctx:
         keep = ctx.enter_context(tc.tile_pool(name="keep", bufs=1))
         raw_pool = ctx.enter_context(tc.tile_pool(name="raw", bufs=RAW_BUFS))
-        grouped_pool = ctx.enter_context(tc.tile_pool(name="grouped", bufs=3))
+        grouped_pool = ctx.enter_context(tc.tile_pool(name="grouped", bufs=4))
         operand_pool = ctx.enter_context(tc.tile_pool(name="operand", bufs=4))
         gate_pool = ctx.enter_context(tc.tile_pool(name="gate", bufs=3))
         rows_pool = ctx.enter_context(tc.tile_pool(name="rows", bufs=2))
@@ -242,17 +242,15 @@ def tile_quest_pb_kernel(
                     in_=o[:].rearrange("p e t -> p t e"),
                 ),
             ]
-            if u == 1:
-                steps.append(lambda: quantise(h2_codes[g], h2_scales[g], h2_grouped[g]))
             return steps
 
         def c2_steps(c, f_cell, i, cand_c):
+            for e in range(2):
+                nc.gpsimd.tensor_mul(out=i[:, e, :], in0=i[:, e, :], in1=cand_c[:, e, :])
             if c == FEATURE_GROUPS - 1:
-                nc.gpsimd.tensor_mul(out=i[:], in0=i[:], in1=cand_c[:])
                 nc.gpsimd.tensor_add(out=f_cell[:], in0=f_cell[:], in1=i[:])
                 return []
             return [
-                lambda: nc.vector.tensor_mul(out=i[:], in0=i[:], in1=cand_c[:]),
                 lambda: nc.vector.tensor_add(out=f_cell[:], in0=f_cell[:], in1=i[:]),
             ]
 
@@ -282,10 +280,12 @@ def tile_quest_pb_kernel(
                     out=rows[:, 2 * pair : 2 * pair + 2, :].rearrange("t j (p e) -> t j p e", e=2),
                     in_=back[:].rearrange("t j e p -> t j p e"),
                 )
-            nc.sync.dma_start(
-                out=dram[:, FEATURES_PER_PANEL * c : FEATURES_PER_PANEL * (c + 1)].rearrange("(t j) x -> t j x", t=P),
-                in_=rows[:],
-            )
+                nc.sync.dma_start(
+                    out=dram[:, FEATURES_PER_PANEL * c : FEATURES_PER_PANEL * (c + 1)].rearrange("(t j) x -> t j x", t=P)[
+                        :, 2 * pair : 2 * pair + 2, :
+                    ],
+                    in_=rows[:, 2 * pair : 2 * pair + 2, :],
+                )
 
         operand = {("z", n): (z_codes[n], z_scales[n]) for n in range(2)}
         grouped = {}
@@ -297,7 +297,7 @@ def tile_quest_pb_kernel(
             loads.extend([(kind, n, part) for part in range(2) if half in (None, part)])
         products.clear()
         back.clear()
-        done = []
+        older, done = [], []
         early = 0
         biases_there = False
 
@@ -305,10 +305,10 @@ def tile_quest_pb_kernel(
             while n_loaded < len(loads) and panels.index(loads[n_loaded][:2]) < panels.index(unused[0]) + RAW_BUFS:
                 load_half(*loads[n_loaded])
                 n_loaded += 1
-                if n_loaded == len(loads):
-                    nc.sync.dma_start(out=b3_all[:], in_=b3.partition_broadcast(P))
                 if loads[n_loaded - 1] == ("o", 3, 1):
                     nc.sync.dma_start(out=cell_rows[:], in_=cell2.rearrange("(t j) x -> t j x", t=P))
+                if loads[n_loaded - 1] == ("i", 1, 1):
+                    nc.sync.dma_start(out=b3_all[:], in_=b3.partition_broadcast(P))
 
             while back and back[0][0] == r:
                 transpose_back_and_store(*back.pop(0)[1:])
@@ -320,7 +320,7 @@ def tile_quest_pb_kernel(
                     nc.vector.tensor_mul(out=live["f", c][:], in0=live["f", c][:], in1=live["cell", c])
 
             mul_kinds = [kind for kind, n, half in mul]
-            vector_banks = () if "w3" in mul_kinds else (1, 3) if len(new) == 2 and ("o" in mul_kinds or new[0][0] == "z") else (3,)
+            vector_banks = (1, 3) if len(new) == 2 and ("o" in mul_kinds or new[0][0] == "z") else (3,)
             for kind, n, half in new:
                 if (kind, n) not in grouped:
                     grouped_tile = grouped_pool.tile([P, PANEL], BF16, align_bytes=64, tag="grouped")
@@ -349,6 +349,9 @@ def tile_quest_pb_kernel(
                     pieces = [(0, PANEL_WORDS // 2), (PANEL_WORDS // 2, PANEL_WORDS // 2)]
                 for piece in pieces:
                     quants.append(lambda p=(kind, n), piece=piece: quantise(*operand[p], grouped[p], *piece))
+            for kind, c, half in older:
+                if kind == "o" and half != 0 and c % 2 == 1:
+                    quants.append(lambda g=c // 2: quantise(h2_codes[g], h2_scales[g], h2_grouped[g]))
             while products or quants:
                 if products:
                     products.pop(0)()
@@ -374,5 +377,5 @@ def tile_quest_pb_kernel(
                 if kind == "i":
                     products.extend(c2_steps(n, live["f", n], live["i", n], cand[n]))
                     back.append((r + 2, n, live["f", n], c2_dram))
-            done = mul
-            early = 1 if mul and mul[0][0] == "i" and products else 0
+            older, done = done, mul
+            early = 0

from contextlib import ExitStack

import concourse.mybir as mybir
from concourse.masks import make_identity

F32 = mybir.dt.float32
BF16 = mybir.dt.bfloat16
I32 = mybir.dt.int32
U32 = mybir.dt.uint32
U8 = mybir.dt.uint8
FP8X4 = mybir.dt.float8_e4m3fn_x4
ACT = mybir.ActivationFunctionType

P = 128
TOKENS = 512
TOKEN_TILES = TOKENS // P
JOINED = 2048
FEATURES = 1024
OUTS = 2048
K_PASS = 512
BANK = 512

PANEL = 4096
PANEL_WORDS = PANEL // 4
SLICES = PANEL_WORDS // P
PANEL_BANKS = 4
FEATURES_PER_PANEL = 256
FEATURE_GROUPS = FEATURES // FEATURES_PER_PANEL
RAW_BUFS = 6

BACK_BEFORE = ((1, 0), (3, 1))
GATES = ("cand", "o", "f", "i")

FLOPS = 2 * TOKENS * JOINED * 4 * FEATURES + 2 * TOKENS * FEATURES * OUTS


def tile_quest_pb_kernel(
    tc, h1, hidden2, cell2, Wf2, bf2, Wi2, bi2, Wc2, bc2, Wo2, bo2, W3, b3, out_0, out_1, out_2
):
    nc = tc.nc
    out3_dram, h2_dram, c2_dram = out_0, out_1, out_2
    gate_weight = {"cand": Wc2, "o": Wo2, "f": Wf2, "i": Wi2}
    gate_bias_dram = {"cand": bc2, "o": bo2, "f": bf2, "i": bi2}
    gate_func = {"cand": ACT.Tanh, "o": ACT.Sigmoid, "f": ACT.Sigmoid, "i": ACT.Sigmoid}

    def whole(*names):
        return [("w3" if name[:-1] == "w" else name[:-1], int(name[-1]), None) for name in names]

    rounds = [
        ([("z", 0, 0), ("z", 1, 0)], []),
        ([("cand", 0, None)], []),
        ([("o", 0, None)], [("cand", 0, 0)]),
        ([("z", 0, 1), ("z", 1, 1)], [("o", 0, 0)]),
        ([("cand", 1, None)], [("cand", 0, 1), ("o", 0, 1)]),
        ([("o", 1, None)], whole("cand1")),
        (whole("cand2", "o2"), whole("o1")),
        (whole("cand3", "o3"), whole("cand2", "o2")),
        (whole("f0", "i0"), whole("cand3", "o3")),
        (whole("f1", "i1"), whole("f0", "i0")),
        (whole("f2", "w0"), whole("f1", "i1")),
        (whole("f3", "i2"), whole("f2", "w0")),
        (whole("i3", "w1"), whole("f3", "i2")),
        (whole("w2", "w3"), whole("i3", "w1")),
        ([], whole("w2", "w3")),
    ]
    new_parts = [part for new, mul in rounds for part in new]
    panels = []
    for kind, n, half in new_parts:
        if (kind, n) not in panels:
            panels.append((kind, n))

    with ExitStack() as ctx:
        keep = ctx.enter_context(tc.tile_pool(name="keep", bufs=1))
        raw_pool = ctx.enter_context(tc.tile_pool(name="raw", bufs=RAW_BUFS))
        grouped_pool = ctx.enter_context(tc.tile_pool(name="grouped", bufs=4))
        operand_pool = ctx.enter_context(tc.tile_pool(name="operand", bufs=4))
        gate_pool = ctx.enter_context(tc.tile_pool(name="gate", bufs=3))
        rows_pool = ctx.enter_context(tc.tile_pool(name="rows", bufs=2))
        y_pool = ctx.enter_context(tc.tile_pool(name="y", bufs=2 * TOKEN_TILES))
        psum = ctx.enter_context(tc.psum_pool(name="psum", bufs=8))
        ctx.enter_context(tc.manual_schedule())

        ident_f32 = keep.tile([P, P], F32)
        make_identity(nc, ident_f32[:])
        ident_bf16 = keep.tile([P, P], BF16)
        make_identity(nc, ident_bf16[:])

        warm = keep.tile([P, 1], F32)

        bias_rows = keep.tile([P, FEATURES_PER_PANEL], BF16)
        gate_bias = keep.tile([P, 2, len(GATES) * FEATURE_GROUPS], F32)
        nc.vector.memset(bias_rows[:].bitcast(I32), 0)
        nc.vector.memset(warm[:], 0.0)
        for gate_no, gate in enumerate(GATES):
            nc.scalar.dma_start(
                out=bias_rows[FEATURE_GROUPS * gate_no : FEATURE_GROUPS * (gate_no + 1), :],
                in_=gate_bias_dram[gate].rearrange("(c x) -> c x", x=FEATURES_PER_PANEL),
            )
        nc.scalar.activation(out=warm[:], in_=warm[:], func=ACT.Sigmoid)

        cell_rows = keep.tile([P, TOKEN_TILES, FEATURES], BF16)
        b3_all = keep.tile([P, OUTS], BF16)

        z_codes = [keep.tile([P, PANEL_WORDS], U32, name="z_codes%d" % n, align_bytes=64) for n in range(2)]
        z_scales = [keep.tile([P, PANEL_WORDS], U8, name="z_scales%d" % n, align_bytes=64) for n in range(2)]
        h2_passes = FEATURES // K_PASS
        h2_grouped = [keep.tile([P, 4 * TOKENS], BF16, name="h2_grouped%d" % g, align_bytes=64) for g in range(h2_passes)]
        h2_codes = [keep.tile([P, TOKENS], U32, name="h2_codes%d" % g, align_bytes=64) for g in range(h2_passes)]
        h2_scales = [keep.tile([P, TOKENS], U8, name="h2_scales%d" % g, align_bytes=64) for g in range(h2_passes)]
        cand = [keep.tile([P, 2, TOKENS], F32, name="cand%d" % c) for c in range(FEATURE_GROUPS)]

        raw = {}
        products = []
        back = []

        def load_half(kind, n, half):
            if (kind, n) not in raw:
                raw_tile = raw_pool.tile([P, PANEL], BF16, tag="raw")
                raw[kind, n] = raw_tile
            columns = slice(half * PANEL // 2, (half + 1) * PANEL // 2)
            if kind == "w3":
                source = W3[BANK * n : BANK * (n + 1), :].rearrange("(j p) k -> p j k", p=P)[:, 2 * half : 2 * half + 2, :]
                target = raw[kind, n][:, columns].rearrange("p (j k) -> p j k", j=2)
            else:
                if kind == "z":
                    rows = (h1, hidden2)[n].rearrange("(p j) k -> p (j k)", j=TOKEN_TILES)
                else:
                    rows = gate_weight[kind][FEATURES_PER_PANEL * n : FEATURES_PER_PANEL * (n + 1), :]
                    rows = rows.rearrange("(p e) k -> p (e k)", e=2)
                source = rows[:, columns]
                target = raw[kind, n][:, columns]
            nc.sync.dma_start(out=target, in_=source)

        def transpose_banks(kind, raw_tile, grouped, banks, vector_banks):
            row_tiles = 2 if kind in gate_weight else 4
            words = raw_tile[:].bitcast(F32).rearrange("p (j g u w) -> p j g u w", j=row_tiles, u=2, w=P)
            grouped_words = grouped[:].bitcast(F32).rearrange("q (s r u) -> q s r u", s=SLICES, u=2)
            for bank_no in banks:
                first, second = divmod(bank_no, 2)
                first_slice = 2 * bank_no if row_tiles == 2 else 4 * second + 2 * first
                flip = psum.tile([P, 2, 2, P], F32, tag="bank")
                for half in range(2):
                    j, g = (first, 2 * second + half) if row_tiles == 2 else (2 * first + half, second)
                    for u in range(2):
                        nc.tensor.transpose(flip[:, half, u, :], words[:, j, g, u, :], ident_f32[:])
                empty_bank = nc.vector.tensor_copy if bank_no in vector_banks else nc.scalar.copy
                empty_bank(
                    out=grouped_words[:, first_slice : first_slice + 2, :, :],
                    in_=flip[:].rearrange("q s u r -> q s r u"),
                )

        def quantise(codes, scales, grouped, first=0, words=None):
            cols = slice(first, first + (words or codes.shape[1]))
            values = slice(4 * cols.start, 4 * cols.stop)
            nc.vector.quantize_mx(out=codes[:, cols].bitcast(FP8X4), scales=scales[:, cols], in_=grouped[:, values])

        def tanh_of_cand():
            if "new_cand" in live:
                c = live.pop("new_cand")
                tanh_cand = gate_pool.tile([P, 2, TOKENS], F32)
                nc.scalar.activation(out=tanh_cand[:], in_=cand[c][:], func=ACT.Tanh)
                live["tanh_cand", c] = tanh_cand

        def gate_matmuls(kind, c, half, codes, scales, gate_out):
            bias_col = FEATURE_GROUPS * GATES.index(kind) + c
            first, width = (0, TOKENS) if half is None else (half * TOKENS // 2, TOKENS // 2)
            both = None
            sums = []
            for e in range(2):
                if half is None or e == 0:
                    both = psum.tile([P, BANK], F32, tag="bank")
                acc = both[:] if half is None else both[:, e * width : (e + 1) * width]
                passes = JOINED // K_PASS
                for g in range(passes):
                    w_cols = slice((passes * e + g) * P, (passes * e + g + 1) * P)
                    z_cols = slice((g % 2) * TOKENS + first, (g % 2) * TOKENS + first + width)
                    nc.tensor.matmul_mx(
                        out=acc,
                        lhsT=codes[:, w_cols].bitcast(FP8X4),
                        lhsT_scale=scales[:, w_cols],
                        rhs=z_codes[g // 2][:, z_cols].bitcast(FP8X4),
                        rhs_scale=z_scales[g // 2][:, z_cols],
                        start=(g == 0),
                        stop=(g == passes - 1),
                    )
                sums.append(acc)
                for n in range(len(sums) if half is None or e == 1 else 0):
                    feature = e if half is None else n
                    nc.scalar.activation(
                        out=gate_out[:, feature, first : first + width],
                        in_=sums.pop(0),
                        func=gate_func[kind],
                        bias=gate_bias[:, feature, bias_col : bias_col + 1],
                        scale=1.0,
                    )
                    if half != 0:
                        tanh_of_cand()
            if kind == "cand" and half != 0:
                live["new_cand"] = c

        def relu_layer_matmuls(n, codes, scales):
            by_tile = out3_dram[:, n * BANK : (n + 1) * BANK].rearrange("(t j) x -> j t x", j=TOKEN_TILES)
            sums = []
            for j in range(TOKEN_TILES):
                if (n, j) in BACK_BEFORE and back:
                    transpose_back_and_store(*back.pop(0)[1:])
                acc = psum.tile([P, BANK], F32, tag="bank")
                tokens = slice(j * P, (j + 1) * P)
                for g in range(h2_passes):
                    w_cols = slice(g * BANK, (g + 1) * BANK)
                    nc.tensor.matmul_mx(
                        out=acc[:],
                        lhsT=h2_codes[g][:, tokens].bitcast(FP8X4),
                        lhsT_scale=h2_scales[g][:, tokens],
                        rhs=codes[:, w_cols].bitcast(FP8X4),
                        rhs_scale=scales[:, w_cols],
                        start=(g == 0),
                        stop=(g == h2_passes - 1),
                    )
                y = y_pool.tile([P, BANK], F32)
                nc.vector.tensor_add(out=y[:], in0=acc[:], in1=b3_all[:, n * BANK : (n + 1) * BANK])
                sums.append(y)
                if j > 0:
                    relu_and_store(n, by_tile[j - 1], sums[j - 1])
                if products and j % 2 == 1:
                    products.pop(0)()
            relu_and_store(n if n < 3 else 0, by_tile[TOKEN_TILES - 1], sums[TOKEN_TILES - 1])

        def relu_and_store(n, dram, y):
            if n == 0:
                nc.vector.tensor_scalar_max(out=y[:], in0=y[:], scalar1=0.0)
            else:
                nc.scalar.activation(out=y[:], in_=y[:], func=ACT.Relu)
            nc.sync.dma_start(out=dram, in_=y[:])

        def h2_steps(c, o, tanh_cand):
            g, u = divmod(c, 2)
            steps = [
                lambda: nc.vector.tensor_mul(out=o[:], in0=o[:], in1=tanh_cand[:]),
                lambda: nc.vector.tensor_copy(
                    out=h2_grouped[g][:].rearrange("p (t v) -> p t v", v=4)[:, :, 2 * u : 2 * u + 2],
                    in_=o[:].rearrange("p e t -> p t e"),
                ),
            ]
            return steps

        def c2_steps(c, f_cell, i, cand_c):
            for e in range(2):
                nc.gpsimd.tensor_mul(out=i[:, e, :], in0=i[:, e, :], in1=cand_c[:, e, :])
            if c == FEATURE_GROUPS - 1:
                nc.gpsimd.tensor_add(out=f_cell[:], in0=f_cell[:], in1=i[:])
                return []
            return [
                lambda: nc.vector.tensor_add(out=f_cell[:], in0=f_cell[:], in1=i[:]),
            ]

        def transpose_biases():
            bias_flip = psum.tile([P, 2, P], BF16, tag="bank")
            by_parity = bias_rows[:].rearrange("r (p e) -> r e p", e=2)
            for e in range(2):
                nc.tensor.transpose(bias_flip[:, e, :], by_parity[:, e, :], ident_bf16[:])
            nc.vector.tensor_copy(out=gate_bias[:], in_=bias_flip[:, :, 0 : len(GATES) * FEATURE_GROUPS])

        def transpose_cell(c):
            cell_flip = psum.tile([P, TOKENS], F32, tag="bank")
            words = cell_rows[:].rearrange("t j x -> t (j x)").bitcast(F32).rearrange("t (j c p) -> t j c p", j=TOKEN_TILES, p=P)
            for j in range(TOKEN_TILES):
                nc.tensor.transpose(cell_flip[:, j * P : (j + 1) * P], words[:, j, c, :], ident_f32[:])
            return cell_flip[:].bitcast(BF16).rearrange("p (t e) -> p e t", e=2)

        def transpose_back_and_store(c, by_feature, dram):
            rows = rows_pool.tile([P, TOKEN_TILES, FEATURES_PER_PANEL], F32)
            for pair in range(TOKEN_TILES // 2):
                back = psum.tile([P, 2, 2, P], F32, tag="bank")
                for half in range(2):
                    j = 2 * pair + half
                    for e in range(2):
                        nc.tensor.transpose(back[:, half, e, :], by_feature[:, e, j * P : (j + 1) * P], ident_f32[:])
                nc.scalar.copy(
                    out=rows[:, 2 * pair : 2 * pair + 2, :].rearrange("t j (p e) -> t j p e", e=2),
                    in_=back[:].rearrange("t j e p -> t j p e"),
                )
                nc.sync.dma_start(
                    out=dram[:, FEATURES_PER_PANEL * c : FEATURES_PER_PANEL * (c + 1)].rearrange("(t j) x -> t j x", t=P)[
                        :, 2 * pair : 2 * pair + 2, :
                    ],
                    in_=rows[:, 2 * pair : 2 * pair + 2, :],
                )

        operand = {("z", n): (z_codes[n], z_scales[n]) for n in range(2)}
        grouped = {}
        live = {}
        n_loaded = 0
        unused = list(panels)
        loads = []
        for kind, n, half in new_parts:
            loads.extend([(kind, n, part) for part in range(2) if half in (None, part)])
        products.clear()
        back.clear()
        older, done = [], []
        early = 0
        biases_there = False

        for r, (new, mul) in enumerate(rounds):
            while n_loaded < len(loads) and panels.index(loads[n_loaded][:2]) < panels.index(unused[0]) + RAW_BUFS:
                load_half(*loads[n_loaded])
                n_loaded += 1
                if loads[n_loaded - 1] == ("o", 3, 1):
                    nc.sync.dma_start(out=cell_rows[:], in_=cell2.rearrange("(t j) x -> t j x", t=P))
                if loads[n_loaded - 1] == ("i", 1, 1):
                    nc.sync.dma_start(out=b3_all[:], in_=b3.partition_broadcast(P))

            while back and back[0][0] == r:
                transpose_back_and_store(*back.pop(0)[1:])

            for n in range(early):
                products.pop(0)()
            for kind, c, half in done:
                if kind == "f":
                    nc.vector.tensor_mul(out=live["f", c][:], in0=live["f", c][:], in1=live["cell", c])

            mul_kinds = [kind for kind, n, half in mul]
            vector_banks = (1, 3) if len(new) == 2 and ("o" in mul_kinds or new[0][0] == "z") else (3,)
            for kind, n, half in new:
                if (kind, n) not in grouped:
                    grouped_tile = grouped_pool.tile([P, PANEL], BF16, align_bytes=64, tag="grouped")
                    grouped[kind, n] = grouped_tile
                banks = range(PANEL_BANKS) if half is None else range(2 * half, 2 * half + 2)
                transpose_banks(kind, raw[kind, n], grouped[kind, n], banks, vector_banks)
                if half != 0:
                    unused.remove((kind, n))
            if mul and not biases_there:
                transpose_biases()
                biases_there = True
            for kind, c, half in mul:
                if kind == "f":
                    live["cell", c] = transpose_cell(c)

            quants = []
            for kind, n, half in new:
                if (kind, n) not in operand:
                    codes = operand_pool.tile([P, PANEL_WORDS], U32, align_bytes=64)
                    scales = operand_pool.tile([P, PANEL_WORDS], U8, align_bytes=64)
                    operand[kind, n] = (codes, scales)
                pieces = [(0, PANEL_WORDS)]
                if kind == "z":
                    pieces = [(g * TOKENS + half * TOKENS // 2, TOKENS // 2) for g in range(2)]
                if (kind, n) == ("cand", 0):
                    pieces = [(0, PANEL_WORDS // 2), (PANEL_WORDS // 2, PANEL_WORDS // 2)]
                for piece in pieces:
                    quants.append(lambda p=(kind, n), piece=piece: quantise(*operand[p], grouped[p], *piece))
            for kind, c, half in older:
                if kind == "o" and half != 0 and c % 2 == 1:
                    quants.append(lambda g=c // 2: quantise(h2_codes[g], h2_scales[g], h2_grouped[g]))
            while products or quants:
                if products:
                    products.pop(0)()
                if quants:
                    quants.pop(0)()

            tanh_of_cand()

            for kind, n, half in mul:
                codes, scales = operand[kind, n]
                if kind == "w3":
                    relu_layer_matmuls(n, codes, scales)
                    continue
                if kind == "cand":
                    live["cand", n] = cand[n]
                elif half != 1:
                    gate_out = gate_pool.tile([P, 2, TOKENS], F32, tag=kind)
                    live[kind, n] = gate_out
                gate_matmuls(kind, n, half, codes, scales, live[kind, n])
                if kind == "o" and half != 0:
                    products.extend(h2_steps(n, live["o", n], live["tanh_cand", n]))
                    back.append((r + 2, n, live["o", n], h2_dram))
                if kind == "i":
                    products.extend(c2_steps(n, live["f", n], live["i", n], cand[n]))
                    back.append((r + 2, n, live["f", n], c2_dram))
            older, done = done, mul
            early = 0
